import numpy as np
import ml_dtypes


def mxq(x, axis, fmt="e4m3"):
    dtype, down = {"e4m3": (ml_dtypes.float8_e4m3fn, 7), "e5m2": (ml_dtypes.float8_e5m2, 14)}[fmt]
    v = np.moveaxis(np.asarray(x, np.float32).astype(ml_dtypes.bfloat16).astype(np.float64), axis, -1)
    blocks = v.reshape(v.shape[:-1] + (-1, 32))
    amax = np.abs(blocks).max(-1, keepdims=True)
    byte = np.maximum(np.where(amax > 0, np.frexp(amax)[1] - 1 + 127, 0) - down, 1)
    scale = np.exp2(byte - 127.0)
    codes = (blocks / scale).astype(np.float32).astype(dtype).astype(np.float64)
    return np.moveaxis((codes * scale).reshape(v.shape), -1, axis)


WIDE = False


def mx_kscale(k):
    if not WIDE:
        return np.ones(k)
    levels = np.array([18, -18])
    if k % 512:
        return np.exp2(np.random.permutation(np.resize(levels, k // 32))).repeat(32)
    a = np.empty((k // 512, 16))
    for p in range(k // 512):
        a[p, :8] = np.random.permutation(np.resize(levels, 8))
        for g in range(8):
            far = levels[np.abs(levels - a[p, g]) >= 10]
            a[p, g + 8] = far[np.random.randint(len(far))]
    return np.exp2(a.ravel()).repeat(32)


BF16 = ml_dtypes.bfloat16


def bf(x):
    return np.asarray(x, np.float32).astype(BF16)


def f64(x):
    return np.asarray(x).astype(np.float64)


B, N, K, H, NUM_IN = 8, 64, 8, 512, 512
T = B * N * K


def setup_inputs():
    s = mx_kscale(T).reshape(B, N, K)[:, :, 0]
    w = mx_kscale(H)
    v = mx_kscale(H)
    u = np.random.standard_normal((B, N, H))
    e = np.random.standard_normal((B, N, K, H))
    h1_0 = bf(np.maximum((u[:, :, None, :] + e) * 0.7, 0.0))
    h_V = bf(np.random.standard_normal((B, N, H)))
    mask = np.random.random((B, N, K)) < 0.9
    W2_0 = bf(np.random.standard_normal((H, H)) * 1.4 / np.sqrt(H))
    b2 = bf(np.random.standard_normal(H) * 0.2)
    W3_0 = bf(np.random.standard_normal((H, H)) * 2.8 / np.sqrt(H))
    b3 = bf(np.random.standard_normal(H) * 0.2)
    g = np.random.standard_normal((B, N, H)) * np.exp2(np.random.randint(-6, 1, (B, N, 1))) * 4.0
    z = f64(h1_0) @ f64(W2_0) + f64(b2)
    mask = mask & (np.min(np.abs(z), axis=-1) > 1e-5)
    return {"h1": bf(f64(h1_0) * s[:, :, None, None]),
            "h_V": h_V,
            "mask_attend": bf(mask),
            "W2": bf(f64(W2_0) / v),
            "b2": b2,
            "W3": bf(f64(W3_0) * v[:, None] / w),
            "b3": b3,
            "z": np.asarray(z, np.float32),
            "grad_out": bf(g / s[:, :, None] * w)}


def reference(h1, h_V, mask_attend, W2, b2, W3, b3, z, grad_out):
    dh = mxq(f64(grad_out).reshape(B * N, H), 1, "e5m2") @ mxq(f64(W3), 1, "e4m3").T
    f = f64(mask_attend)[..., None] / K
    dz1 = dh.reshape(B, N, 1, H) * f * (f64(z) > 0.0)
    dz1 = dz1.reshape(T, H)
    dh1 = mxq(dz1, 1, "e5m2") @ mxq(f64(W2), 1, "e4m3").T
    dW2 = mxq(f64(h1).reshape(T, H), 0, "e4m3").T @ mxq(dz1, 0, "e5m2")
    return dh1.reshape(B, N, K, H), dW2

@@ -1,0 +1,360 @@
+from contextlib import ExitStack
+
+import concourse.mybir as mybir
+from concourse.masks import make_identity
+
+F32 = mybir.dt.float32
+BF16 = mybir.dt.bfloat16
+U32 = mybir.dt.uint32
+U8 = mybir.dt.uint8
+E4M3 = mybir.dt.float8_e4m3fn_x4
+E5M2 = mybir.dt.float8_e5m2_x4
+ALU = mybir.AluOpType
+ACT = mybir.ActivationFunctionType
+
+P = 128
+H = 512
+NODES = 512
+EDGES = 4096
+GROUPS = 8
+J = 4
+FMAX = (2.0 - 2.0 ** -23) * 2.0 ** 127
+
+FLOPS = 2 * H * H * (NODES + EDGES + EDGES)
+BYTES = 2 * (EDGES * H + EDGES + 2 * H * H + NODES * H) + 4 * (EDGES * H + EDGES * H + H * H)
+
+
+def tile_mpnnlayer_pb_v_kernel(tc, h1, h_V, mask_attend, W2, b2, W3, b3, z, grad_out, out_0, out_1):
+    nc = tc.nc
+    h1_v = h1.rearrange("b n k w -> (b n k) w").rearrange("(g p j) w -> p g j w", p=P, j=J)
+    z_v = z.rearrange("b n k w -> (b n k) w").rearrange("(g p j) w -> p g j w", p=P, j=J)
+    o_v = out_0.rearrange("b n k w -> (b n k) w").rearrange("(g p j) w -> p g j w", p=P, j=J)
+    mask_v = mask_attend.rearrange("b n k -> (b n k)").rearrange("(g c) -> g c", g=GROUPS)
+    grad_v = grad_out.rearrange("b n w -> (b n) w").rearrange("(t p) w -> p t w", p=P)
+    w2_v = W2.rearrange("(b r v) w -> r b v w", b=2, v=2)
+    w3_v = W3.rearrange("(b r v) w -> r b v w", b=2, v=2)
+
+    with ExitStack() as ctx:
+        ctx.enter_context(tc.manual_schedule())
+        sb = ctx.enter_context(tc.tile_pool(name="sb", bufs=1))
+        ps = ctx.enter_context(tc.psum_pool(name="ps", bufs=2))
+
+        def new(shape, dtype, tag, bufs=1):
+            return sb.tile(shape, dtype, name=tag, tag=tag, bufs=bufs, align_bytes=64)
+
+        def bank(tag):
+            return ps.tile([P, 512], F32, name=tag, tag=tag, bufs=2)
+
+        ident = new([P, P], F32, "ident")
+        make_identity(nc, ident[:])
+        mk = new([P, H], BF16, "mk")
+        nc.vector.memset(mk[:], 0.0)
+        nc.scalar.dma_start(out=mk[0:GROUPS, :], in_=mask_v)
+
+        g_raw = new([P, 4, H], BF16, "g_raw")
+        w3_raw = new([P, J, H], BF16, "w3_raw")
+        w2_raw = new([P, J, H], BF16, "w2_raw")
+
+        def load_w(raw, view, b):
+            nc.sync.dma_start(out=raw[:, 2 * b:2 * b + 2, :], in_=view[:, b])
+
+        z_t = {}
+        h1_t = {}
+
+        def load_z(g):
+            if g < GROUPS:
+                z_t[g] = new([P, J, H], F32, "z", 6)
+                nc.sync.dma_start(out=z_t[g][:], in_=z_v[:, g])
+
+        def load_h1(g):
+            if g < GROUPS:
+                h1_t[g] = new([P, J, H], BF16, "h1", 6)
+                nc.sync.dma_start(out=h1_t[g][:], in_=h1_v[:, g])
+
+        nc.sync.dma_start(out=g_raw[:, 0, :], in_=grad_v[:, 0, :])
+        load_w(w3_raw, w3_v, 0)
+        load_w(w3_raw, w3_v, 1)
+        load_z(0)
+        load_h1(0)
+        nc.sync.dma_start(out=g_raw[:, 1:4, :], in_=grad_v[:, 1:4, :])
+        load_w(w2_raw, w2_v, 0)
+        load_w(w2_raw, w2_v, 1)
+        for g in range(1, 6):
+            load_z(g)
+            load_h1(g)
+
+        def transpose_words(dst, words):
+            for u in range(2):
+                nc.tensor.transpose(dst[:, u, :], words[:, u:256:2], ident[:])
+
+        def words_of(tile3, j):
+            return tile3[:, j, :].bitcast(F32)
+
+        g_codes = new([P, 2 * NODES], U32, "g_codes")
+        g_scl = new([P, 2 * NODES], U8, "g_scl")
+
+        def g_transpose(t, tag):
+            b = bank(tag)
+            bv = b[:].rearrange("p (v u r) -> p v u r", u=2, r=P)
+            transpose_words(bv[:, 0], words_of(g_raw, t))
+            return bv
+
+        def g_copy(copy, bv):
+            gt = new([P, 2 * P * 4], BF16, "gt", 4)
+            copy(
+                out=gt[:].bitcast(F32).rearrange("p (r d u) -> p r d u", d=2, u=2),
+                in_=bv[:, 0].rearrange("p u r -> p r u").unsqueeze(2).to_broadcast([P, P, 2, 2]),
+            )
+            return gt
+
+        def g_quant(t, gt):
+            cols = slice(256 * t, 256 * (t + 1))
+            nc.vector.quantize_mx(out=g_codes[:, cols].bitcast(E5M2), scales=g_scl[:, cols], in_=gt[:])
+
+        def w_bank(raw, b, tag):
+            bk = bank(tag)
+            bv = bk[:].rearrange("p (v u r) -> p v u r", u=2, r=P)
+            for v in range(2):
+                transpose_words(bv[:, v], words_of(raw, 2 * b + v))
+            return bv
+
+        def w_copy(copy, dst, b, bv):
+            copy(
+                out=dst[:].bitcast(F32).rearrange("p (b r v u) -> p b r v u", b=2, v=2, u=2)[:, b],
+                in_=bv.rearrange("p v u r -> p r v u"),
+            )
+
+        def w_quant(codes, scl, dst, b):
+            cols = slice(256 * b, 256 * (b + 1))
+            nc.vector.quantize_mx(out=codes[:, cols].bitcast(E4M3), scales=scl[:, cols], in_=dst[:, 1024 * b:1024 * (b + 1)])
+
+        vcopy = nc.vector.tensor_copy
+        scopy = nc.scalar.copy
+
+        gb0 = g_transpose(0, "acc")
+        gt0 = g_copy(vcopy, gb0)
+        w3_t = new([P, J * H], BF16, "w3_t")
+        w3_codes = new([P, H], U32, "w3_codes")
+        w3_scl = new([P, H], U8, "w3_scl")
+        w_copy(scopy, w3_t, 0, w_bank(w3_raw, 0, "mm"))
+        g_quant(0, gt0)
+        w_quant(w3_codes, w3_scl, w3_t, 0)
+        w_copy(scopy, w3_t, 1, w_bank(w3_raw, 1, "mm"))
+
+        mb = bank("acc")
+        mv = mb[:].rearrange("p (v u r) -> p v u r", u=2, r=P)
+        transpose_words(mv[:, 0], mk[:].bitcast(F32))
+        m_t = new([P, GROUPS * J], BF16, "m_t")
+        vcopy(
+            out=m_t[:].bitcast(F32).rearrange("p (g u) -> p g u", u=2),
+            in_=mv[:, 0, :, 0:GROUPS].rearrange("p u g -> p g u"),
+        )
+        thr = new([P, GROUPS * J], F32, "thr")
+        nc.vector.tensor_scalar(out=thr[:], in0=m_t[:], scalar1=-FMAX, scalar2=FMAX, op0=ALU.mult, op1=ALU.add)
+        w_quant(w3_codes, w3_scl, w3_t, 1)
+
+        dh_t = {}
+
+        def dh_matmul(g):
+            if g < GROUPS:
+                dh_t[g] = bank("dh")
+                cols = slice(P * g, P * (g + 1))
+                nc.tensor.matmul_mx(
+                    out=dh_t[g][:],
+                    lhsT=g_codes[:, cols].bitcast(E5M2), lhsT_scale=g_scl[:, cols],
+                    rhs=w3_codes[:].bitcast(E4M3), rhs_scale=w3_scl[:],
+                    start=True, stop=True,
+                )
+
+        dh_matmul(0)
+        dh_matmul(1)
+
+        dz_t, dzi_t, dzc_t, dzs_t, h1i_t, h1c_t, h1s_t = {}, {}, {}, {}, {}, {}, {}
+        tr_t, dzT_t, tc_t, ts_t, o_t = {}, {}, {}, {}, {}
+        w2_codes = new([P, H], U32, "w2_codes")
+        w2_scl = new([P, H], U8, "w2_scl")
+
+        def h1_interleave(g):
+            if g < GROUPS:
+                h1i_t[g] = new([P, J * H], BF16, "h1i", 2)
+                nc.gpsimd.tensor_scalar(
+                    out=h1i_t[g][:].rearrange("p (w j) -> p w j", j=J),
+                    in0=h1_t[g][:].rearrange("p j w -> p w j"),
+                    scalar1=1.0, scalar2=0.0, op0=ALU.mult, op1=ALU.add,
+                )
+
+        def h1_quant(g):
+            h1c_t[g] = new([P, H], U32, "h1c", 8)
+            h1s_t[g] = new([P, H], U8, "h1s", 8)
+            nc.vector.quantize_mx(out=h1c_t[g][:].bitcast(E4M3), scales=h1s_t[g][:], in_=h1i_t[g][:])
+
+        def dz_compute(g, j):
+            if j == 0:
+                dz_t[g] = new([P, J, H], BF16, "dz", 3)
+            nc.vector.scalar_tensor_tensor(
+                out=dz_t[g][:, j, :], in0=z_t[g][:, j, :], scalar=thr[:, J * g + j:J * g + j + 1],
+                in1=dh_t[g][:], op0=ALU.is_gt, op1=ALU.mult,
+            )
+
+        def dz_interleave(copy, g, half):
+            if half == 0:
+                dzi_t[g] = new([P, J * H], BF16, "dzi", 2)
+            cols = slice(256 * half, 256 * (half + 1))
+            copy(
+                out=dzi_t[g][:].rearrange("p (w j) -> p w j", j=J)[:, cols, :],
+                in_=dz_t[g][:].rearrange("p j w -> p w j")[:, cols, :],
+            )
+
+        def dz_quant(g):
+            dzc_t[g] = new([P, H], U32, "dzc", 8)
+            dzs_t[g] = new([P, H], U8, "dzs", 8)
+            nc.vector.quantize_mx(out=dzc_t[g][:].bitcast(E5M2), scales=dzs_t[g][:], in_=dzi_t[g][:])
+
+        def dzT_transpose(g, h):
+            bk = bank("tr")
+            tr_t[g, h] = bk[:].rearrange("p (v u r) -> p v u r", u=2, r=P)
+            for v in range(2):
+                transpose_words(tr_t[g, h][:, v], words_of(dz_t[g], 2 * h + v))
+
+        def dzT_copy(g, h):
+            dzT_t[g, h] = new([P, 2 * P * 4], BF16, "dzT", 3)
+            (scopy if h == 1 and g % 2 == 1 and g < GROUPS - 1 else vcopy)(
+                out=dzT_t[g, h][:].bitcast(F32).rearrange("p (v r u) -> p v r u", r=P, u=2),
+                in_=tr_t[g, h].rearrange("p v u r -> p v r u"),
+            )
+
+        def dzT_quant(g, h):
+            tc_t[g, h] = new([P, 2 * P], U32, "tcod", 3)
+            ts_t[g, h] = new([P, 2 * P], U8, "tscl", 3)
+            nc.vector.quantize_mx(out=tc_t[g, h][:].bitcast(E5M2), scales=ts_t[g, h][:], in_=dzT_t[g, h][:])
+
+        def out0_matmul(g, h, v):
+            bk = bank("mm")
+            cols = slice(P * v, P * (v + 1))
+            nc.tensor.matmul_mx(
+                out=bk[:],
+                lhsT=tc_t[g, h][:, cols].bitcast(E5M2), lhsT_scale=ts_t[g, h][:, cols],
+                rhs=w2_codes[:].bitcast(E4M3), rhs_scale=w2_scl[:],
+                start=True, stop=True,
+            )
+            return bk
+
+        def out0_copy_s(g, h, v, bk):
+            nc.scalar.activation(out=o_t[g][:, 2 * h + v, :], in_=bk[:], func=ACT.Copy, scale=0.125)
+
+        def out0_copy_v(g, h, v, bk):
+            nc.vector.tensor_scalar(out=o_t[g][:, 2 * h + v, :], in0=bk[:], scalar1=0.125, scalar2=None, op0=ALU.mult)
+
+        def out0_half(g, h, emits=None):
+            if h == 0:
+                o_t[g] = new([P, J, H], F32, "o", 3)
+            banks = [out0_matmul(g, h, v) for v in range(2)]
+            for v in range(2):
+                (out0_copy_s if emits is None else emits[v])(g, h, v, banks[v])
+
+        acc = {}
+
+        def out1_pass(g, m):
+            if g == 0:
+                acc[m] = bank("acc" if m < 2 else "dh")
+            cols = slice(P * m, P * (m + 1))
+            nc.tensor.matmul_mx(
+                out=acc[m][:],
+                lhsT=h1c_t[g][:, cols].bitcast(E4M3), lhsT_scale=h1s_t[g][:, cols],
+                rhs=dzc_t[g][:].bitcast(E5M2), rhs_scale=dzs_t[g][:],
+                start=(g == 0), stop=(g == GROUPS - 1),
+            )
+
+        h1_interleave(0)
+        h1_interleave(1)
+        last = GROUPS - 1
+
+        def store(g, lo, hi):
+            nc.sync.dma_start(out=o_v[:, g, lo:hi], in_=o_t[g][:, lo:hi, :])
+
+        for g in range(last):
+            dz_compute(g, 0)
+            dz_compute(g, 1)
+            dzT_transpose(g, 0)
+            if g == 0:
+                gts = [g_copy(scopy, g_transpose(t, "acc")) for t in range(1, 4)]
+                w2_t = new([P, J * H], BF16, "w2_t")
+                for b in range(2):
+                    w_copy(scopy, w2_t, b, w_bank(w2_raw, b, "mm"))
+            if g > 0:
+                dzT_copy(g - 1, 1)
+                out0_half(g - 1, 0)
+            if g > 1:
+                for m in range(2):
+                    out1_pass(g - 2, m)
+            dz_compute(g, 2)
+            dzT_copy(g, 0)
+            dz_compute(g, 3)
+            dzT_transpose(g, 1)
+            if g == 0:
+                for t in range(1, 4):
+                    g_quant(t, gts[t - 1])
+                for b in range(2):
+                    w_quant(w2_codes, w2_scl, w2_t, b)
+            dh_matmul(g + 2)
+            dz_interleave(scopy, g, 0)
+            load_z(g + 6)
+            load_h1(g + 6)
+            if g > 0:
+                dzT_quant(g - 1, 1)
+                out0_half(g - 1, 1)
+                store(g - 1, 0, J)
+            dz_interleave(scopy, g, 1)
+            dzT_quant(g, 0)
+            if g > 0:
+                dz_quant(g - 1)
+            h1_quant(g)
+            if g + 2 < GROUPS:
+                h1_interleave(g + 2)
+            if g == last - 1:
+                h1_quant(last)
+                for k in range(5):
+                    out1_pass(k, 2)
+
+        g = last
+        dz_compute(g, 0)
+        dz_compute(g, 1)
+        dzT_transpose(g, 0)
+        dzT_copy(g - 1, 1)
+        out0_half(g - 1, 0)
+        for m in range(2):
+            out1_pass(g - 2, m)
+        dzT_quant(g - 1, 1)
+        dz_quant(g - 1)
+        dz_compute(g, 2)
+        out0_half(g - 1, 1)
+        store(g - 1, 0, J)
+        dzT_copy(g, 0)
+        dz_compute(g, 3)
+        dzT_transpose(g, 1)
+        dz_interleave(scopy, g, 0)
+        dzT_quant(g, 0)
+        out0_half(g, 0)
+        store(g, 0, 2)
+        dz_interleave(vcopy, g, 1)
+        for k in range(5):
+            out1_pass(k, 3)
+        dzT_copy(g, 1)
+        for m in range(2):
+            out1_pass(g - 1, m)
+        for k in (g - 2, g - 1):
+            for m in (2, 3):
+                out1_pass(k, m)
+        dz_quant(g)
+        dzT_quant(g, 1)
+        o1 = new([P, 4, H], F32, "o1")
+        o1_v = out_1.rearrange("(m p) w -> p m w", p=P)
+        for m in range(4):
+            out1_pass(g, m)
+            if m % 2 == 0:
+                nc.scalar.activation(out=o1[:, m, :], in_=acc[m][:], func=ACT.Copy, scale=0.125)
+            else:
+                nc.vector.tensor_scalar(out=o1[:, m, :], in0=acc[m][:], scalar1=0.125, scalar2=None, op0=ALU.mult)
+                nc.sync.dma_start(out=o1_v[:, m - 1:m + 1], in_=o1[:, m - 1:m + 1, :])
+        out0_half(g, 1, emits=(out0_copy_s, out0_copy_v))
+        store(g, 2, 4)

@@ -18,6 +18,16 @@ NODES = 512
 EDGES = 4096
 GROUPS = 8
 J = 4
+TCS = (1, 2, 3, 4, 5, 6)
+TI = 256
+CS = 2
+ILW = 2
+SILC = True
+GS = 4
+NIL = 6
+SW = 4
+ZB = 5
+OB = 4
 FMAX = (2.0 - 2.0 ** -23) * 2.0 ** 127
 
 FLOPS = 2 * H * H * (NODES + EDGES + EDGES)
@@ -43,13 +53,14 @@ def tile_mpnnlayer_pb_v_kernel(tc, h1, h_V, mask_attend, W2, b2, W3, b3, z, grad
             return sb.tile(shape, dtype, name=tag, tag=tag, bufs=bufs, align_bytes=64)
 
         def bank(tag):
-            return ps.tile([P, 512], F32, name=tag, tag=tag, bufs=2)
+            return ps.tile([P, 512], F32, name=tag, tag=tag, bufs={"acc": 3, "mm": 2}.get(tag, 1))
 
         ident = new([P, P], F32, "ident")
         make_identity(nc, ident[:])
+        ident16 = new([P, P], BF16, "ident16")
+        nc.vector.tensor_copy(out=ident16[:], in_=ident[:])
         mk = new([P, H], BF16, "mk")
         nc.vector.memset(mk[:], 0.0)
-        nc.scalar.dma_start(out=mk[0:GROUPS, :], in_=mask_v)
 
         g_raw = new([P, 4, H], BF16, "g_raw")
         w3_raw = new([P, J, H], BF16, "w3_raw")
@@ -63,23 +74,26 @@ def tile_mpnnlayer_pb_v_kernel(tc, h1, h_V, mask_attend, W2, b2, W3, b3, z, grad
 
         def load_z(g):
             if g < GROUPS:
-                z_t[g] = new([P, J, H], F32, "z", 6)
+                z_t[g] = new([P, J, H], F32, "z", ZB)
                 nc.sync.dma_start(out=z_t[g][:], in_=z_v[:, g])
 
         def load_h1(g):
             if g < GROUPS:
-                h1_t[g] = new([P, J, H], BF16, "h1", 6)
+                h1_t[g] = new([P, J, H], BF16, "h1", ZB)
                 nc.sync.dma_start(out=h1_t[g][:], in_=h1_v[:, g])
 
-        nc.sync.dma_start(out=g_raw[:, 0, :], in_=grad_v[:, 0, :])
         load_w(w3_raw, w3_v, 0)
         load_w(w3_raw, w3_v, 1)
+        nc.sync.dma_start(out=g_raw[:, 0, :], in_=grad_v[:, 0, :])
+        nc.sync.dma_start(out=mk[0:GROUPS, :], in_=mask_v)
         load_z(0)
-        load_h1(0)
         nc.sync.dma_start(out=g_raw[:, 1:4, :], in_=grad_v[:, 1:4, :])
         load_w(w2_raw, w2_v, 0)
         load_w(w2_raw, w2_v, 1)
-        for g in range(1, 6):
+        load_z(1)
+        load_h1(1)
+        load_h1(0)
+        for g in range(2, ZB):
             load_z(g)
             load_h1(g)
 
@@ -99,17 +113,23 @@ def tile_mpnnlayer_pb_v_kernel(tc, h1, h_V, mask_attend, W2, b2, W3, b3, z, grad
             transpose_words(bv[:, 0], words_of(g_raw, t))
             return bv
 
-        def g_copy(copy, bv):
-            gt = new([P, 2 * P * 4], BF16, "gt", 4)
+        def g_tile():
+            return new([P, 2 * P * 4], BF16, "gt", 4)
+
+        def g_copy(copy, gt, bv, half):
+            rows = slice(64 * half, 64 * half + 64) if half < 2 else slice(0, P)
+            n = P if half == 2 else 64
             copy(
-                out=gt[:].bitcast(F32).rearrange("p (r d u) -> p r d u", d=2, u=2),
-                in_=bv[:, 0].rearrange("p u r -> p r u").unsqueeze(2).to_broadcast([P, P, 2, 2]),
+                out=gt[:].bitcast(F32).rearrange("p (r d u) -> p r d u", d=2, u=2)[:, rows],
+                in_=bv[:, 0, :, rows].rearrange("p u r -> p r u").unsqueeze(2).to_broadcast([P, n, 2, 2]),
             )
             return gt
 
-        def g_quant(t, gt):
-            cols = slice(256 * t, 256 * (t + 1))
-            nc.vector.quantize_mx(out=g_codes[:, cols].bitcast(E5M2), scales=g_scl[:, cols], in_=gt[:])
+        def g_quant(t, gt, half):
+            lo, hi = (0, 256) if half == 2 else (128 * half, 128 * half + 128)
+            nc.vector.quantize_mx(
+                out=g_codes[:, 256 * t + lo:256 * t + hi].bitcast(E5M2), scales=g_scl[:, 256 * t + lo:256 * t + hi],
+                in_=gt[:, 4 * lo:4 * hi])
 
         def w_bank(raw, b, tag):
             bk = bank(tag)
@@ -131,19 +151,20 @@ def tile_mpnnlayer_pb_v_kernel(tc, h1, h_V, mask_attend, W2, b2, W3, b3, z, grad
         vcopy = nc.vector.tensor_copy
         scopy = nc.scalar.copy
 
-        gb0 = g_transpose(0, "acc")
-        gt0 = g_copy(vcopy, gb0)
         w3_t = new([P, J * H], BF16, "w3_t")
         w3_codes = new([P, H], U32, "w3_codes")
         w3_scl = new([P, H], U8, "w3_scl")
         w_copy(scopy, w3_t, 0, w_bank(w3_raw, 0, "mm"))
-        g_quant(0, gt0)
-        w_quant(w3_codes, w3_scl, w3_t, 0)
-        w_copy(scopy, w3_t, 1, w_bank(w3_raw, 1, "mm"))
-
+        w_copy(vcopy, w3_t, 1, w_bank(w3_raw, 1, "mm"))
+        gb0 = g_transpose(0, "acc")
+        gt0 = g_tile()
+        g_copy(scopy, gt0, gb0, 0)
         mb = bank("acc")
         mv = mb[:].rearrange("p (v u r) -> p v u r", u=2, r=P)
         transpose_words(mv[:, 0], mk[:].bitcast(F32))
+        w_quant(w3_codes, w3_scl, w3_t, 0)
+        w_quant(w3_codes, w3_scl, w3_t, 1)
+        g_quant(0, gt0, 0)
         m_t = new([P, GROUPS * J], BF16, "m_t")
         vcopy(
             out=m_t[:].bitcast(F32).rearrange("p (g u) -> p g u", u=2),
@@ -151,7 +172,6 @@ def tile_mpnnlayer_pb_v_kernel(tc, h1, h_V, mask_attend, W2, b2, W3, b3, z, grad
         )
         thr = new([P, GROUPS * J], F32, "thr")
         nc.vector.tensor_scalar(out=thr[:], in0=m_t[:], scalar1=-FMAX, scalar2=FMAX, op0=ALU.mult, op1=ALU.add)
-        w_quant(w3_codes, w3_scl, w3_t, 1)
 
         dh_t = {}
 
@@ -167,21 +187,32 @@ def tile_mpnnlayer_pb_v_kernel(tc, h1, h_V, mask_attend, W2, b2, W3, b3, z, grad
                 )
 
         dh_matmul(0)
-        dh_matmul(1)
+        g_copy(scopy, gt0, gb0, 1)
+        gts = {}
 
         dz_t, dzi_t, dzc_t, dzs_t, h1i_t, h1c_t, h1s_t = {}, {}, {}, {}, {}, {}, {}
         tr_t, dzT_t, tc_t, ts_t, o_t = {}, {}, {}, {}, {}
         w2_codes = new([P, H], U32, "w2_codes")
         w2_scl = new([P, H], U8, "w2_scl")
 
-        def h1_interleave(g):
-            if g < GROUPS:
-                h1i_t[g] = new([P, J * H], BF16, "h1i", 2)
-                nc.gpsimd.tensor_scalar(
-                    out=h1i_t[g][:].rearrange("p (w j) -> p w j", j=J),
-                    in0=h1_t[g][:].rearrange("p j w -> p w j"),
-                    scalar1=1.0, scalar2=0.0, op0=ALU.mult, op1=ALU.add,
-                )
+        last_codes = [None]
+
+        def h1_interleave(on_gpsimd, g):
+            h1i_t[g] = new([P, J * H], BF16, "h1i", 2)
+            out = h1i_t[g][:].rearrange("p (w j) -> p w j", j=J)
+            in_ = h1_t[g][:].rearrange("p j w -> p w j")
+            if on_gpsimd:
+                nc.gpsimd.tensor_scalar(out=out, in0=in_, scalar1=1.0, scalar2=0.0, op0=ALU.mult, op1=ALU.add)
+            else:
+                for k in range(2):
+                    cols = slice(256 * k, 256 * (k + 1))
+                    nc.scalar.copy(out=out[:, cols], in_=in_[:, cols])
+
+        token = new([P, 1], U32, "token")
+
+        def h1_step(g):
+            nc.gpsimd.tensor_copy(out=token[:], in_=last_codes[0][:, 0:1])
+            h1_interleave(True, g)
 
         def h1_quant(g):
             h1c_t[g] = new([P, H], U32, "h1c", 8)
@@ -196,14 +227,31 @@ def tile_mpnnlayer_pb_v_kernel(tc, h1, h_V, mask_attend, W2, b2, W3, b3, z, grad
                 in1=dh_t[g][:], op0=ALU.is_gt, op1=ALU.mult,
             )
 
-        def dz_interleave(copy, g, half):
-            if half == 0:
+        def dz_interleave_pe(copy, g):
+            lo = H - 128 * ILW
+            if ILW == 0 or g >= NIL:
+                return
+            bk = ps.tile([P, 1024], BF16, name="il", tag="il", bufs=1)
+            for k in range(ILW):
+                w0 = lo + 128 * k
+                nc.tensor.matmul(
+                    out=bk[:, 512 * k:512 * (k + 1)], lhsT=ident16[:],
+                    rhs=dz_t[g][:, :, w0:w0 + 128].rearrange("p j w -> p w j"),
+                    start=True, stop=True,
+                )
+            copy(out=dzi_t[g][:, 4 * lo:4 * H], in_=bk[:, 0:512 * ILW])
+
+        def dz_interleave(copy, g, lo, hi):
+            if hi == lo:
+                return
+            if g not in dzi_t:
                 dzi_t[g] = new([P, J * H], BF16, "dzi", 2)
-            cols = slice(256 * half, 256 * (half + 1))
-            copy(
-                out=dzi_t[g][:].rearrange("p (w j) -> p w j", j=J)[:, cols, :],
-                in_=dz_t[g][:].rearrange("p j w -> p w j")[:, cols, :],
-            )
+            out = dzi_t[g][:].rearrange("p (w j) -> p w j", j=J)[:, lo:hi, :]
+            in_ = dz_t[g][:].rearrange("p j w -> p w j")[:, lo:hi, :]
+            if copy == "g":
+                nc.gpsimd.tensor_scalar(out=out, in0=in_, scalar1=1.0, scalar2=0.0, op0=ALU.mult, op1=ALU.add)
+            else:
+                copy(out=out, in_=in_)
 
         def dz_quant(g):
             dzc_t[g] = new([P, H], U32, "dzc", 8)
@@ -218,7 +266,7 @@ def tile_mpnnlayer_pb_v_kernel(tc, h1, h_V, mask_attend, W2, b2, W3, b3, z, grad
 
         def dzT_copy(g, h):
             dzT_t[g, h] = new([P, 2 * P * 4], BF16, "dzT", 3)
-            (scopy if h == 1 and g % 2 == 1 and g < GROUPS - 1 else vcopy)(
+            (scopy if h == 1 and g in TCS else vcopy)(
                 out=dzT_t[g, h][:].bitcast(F32).rearrange("p (v r u) -> p v r u", r=P, u=2),
                 in_=tr_t[g, h].rearrange("p v u r -> p v r u"),
             )
@@ -227,6 +275,7 @@ def tile_mpnnlayer_pb_v_kernel(tc, h1, h_V, mask_attend, W2, b2, W3, b3, z, grad
             tc_t[g, h] = new([P, 2 * P], U32, "tcod", 3)
             ts_t[g, h] = new([P, 2 * P], U8, "tscl", 3)
             nc.vector.quantize_mx(out=tc_t[g, h][:].bitcast(E5M2), scales=ts_t[g, h][:], in_=dzT_t[g, h][:])
+            last_codes[0] = tc_t[g, h]
 
         def out0_matmul(g, h, v):
             bk = bank("mm")
@@ -247,7 +296,7 @@ def tile_mpnnlayer_pb_v_kernel(tc, h1, h_V, mask_attend, W2, b2, W3, b3, z, grad
 
         def out0_half(g, h, emits=None):
             if h == 0:
-                o_t[g] = new([P, J, H], F32, "o", 3)
+                o_t[g] = new([P, J, H], F32, "o", OB)
             banks = [out0_matmul(g, h, v) for v in range(2)]
             for v in range(2):
                 (out0_copy_s if emits is None else emits[v])(g, h, v, banks[v])
@@ -256,7 +305,7 @@ def tile_mpnnlayer_pb_v_kernel(tc, h1, h_V, mask_attend, W2, b2, W3, b3, z, grad
 
         def out1_pass(g, m):
             if g == 0:
-                acc[m] = bank("acc" if m < 2 else "dh")
+                acc[m] = bank("acc" if m < 3 else "il")
             cols = slice(P * m, P * (m + 1))
             nc.tensor.matmul_mx(
                 out=acc[m][:],
@@ -265,96 +314,128 @@ def tile_mpnnlayer_pb_v_kernel(tc, h1, h_V, mask_attend, W2, b2, W3, b3, z, grad
                 start=(g == 0), stop=(g == GROUPS - 1),
             )
 
-        h1_interleave(0)
-        h1_interleave(1)
         last = GROUPS - 1
+        c0 = 256
 
         def store(g, lo, hi):
             nc.sync.dma_start(out=o_v[:, g, lo:hi], in_=o_t[g][:, lo:hi, :])
 
-        for g in range(last):
+        dz_compute(0, 0)
+        dz_compute(0, 1)
+        for t in (1, 2, 3):
+            gts[t] = g_copy(scopy if t < GS else vcopy, g_tile(), g_transpose(t, "acc"), 2)
+        dzT_transpose(0, 0)
+        w2_t = new([P, J * H], BF16, "w2_t")
+        for b in range(2):
+            w_copy(scopy if b < CS else vcopy, w2_t, b, w_bank(w2_raw, b, "mm"))
+        dz_compute(0, 2)
+        dzT_copy(0, 0)
+        g_quant(0, gt0, 1)
+        dz_compute(0, 3)
+        dh_matmul(1)
+        dzT_transpose(0, 1)
+        load_z(ZB)
+        load_h1(ZB)
+        dz_interleave(scopy, 0, 0, c0)
+        dz_interleave_pe(scopy, 0)
+        dzT_quant(0, 0)
+        for b in range(2):
+            w_quant(w2_codes, w2_scl, w2_t, b)
+        out0_half(0, 0)
+        g_quant(1, gts[1], 2)
+        dzT_copy(0, 1)
+        dz_interleave(scopy, 0, c0, H - 128 * ILW)
+        for t in (2, 3):
+            g_quant(t, gts[t], 2)
+        dzT_quant(0, 1)
+        out0_half(0, 1)
+        store(0, 0, J)
+        h1_interleave(False, 0)
+
+        for g in range(1, last):
+            prev1 = g > 1
+            h1_step(g)
+            if prev1 and g - 1 not in TCS:
+                dzT_copy(g - 1, 1)
             dz_compute(g, 0)
             dz_compute(g, 1)
             dzT_transpose(g, 0)
-            if g == 0:
-                gts = [g_copy(scopy, g_transpose(t, "acc")) for t in range(1, 4)]
-                w2_t = new([P, J * H], BF16, "w2_t")
-                for b in range(2):
-                    w_copy(scopy, w2_t, b, w_bank(w2_raw, b, "mm"))
-            if g > 0:
-                dzT_copy(g - 1, 1)
-                out0_half(g - 1, 0)
-            if g > 1:
+            if prev1:
+                if g > 2:
+                    out0_half(g - 1, 0)
                 for m in range(2):
                     out1_pass(g - 2, m)
             dz_compute(g, 2)
-            dzT_copy(g, 0)
             dz_compute(g, 3)
+            dzT_copy(g, 0)
+            dh_matmul(g + 1)
             dzT_transpose(g, 1)
-            if g == 0:
-                for t in range(1, 4):
-                    g_quant(t, gts[t - 1])
-                for b in range(2):
-                    w_quant(w2_codes, w2_scl, w2_t, b)
-            dh_matmul(g + 2)
-            dz_interleave(scopy, g, 0)
-            load_z(g + 6)
-            load_h1(g + 6)
-            if g > 0:
+            dz_interleave(scopy, g, 0, c0)
+            if g in TCS:
+                dzT_copy(g, 1)
+            load_z(g + ZB)
+            load_h1(g + ZB)
+            if prev1:
                 dzT_quant(g - 1, 1)
                 out0_half(g - 1, 1)
                 store(g - 1, 0, J)
-            dz_interleave(scopy, g, 1)
-            dzT_quant(g, 0)
-            if g > 0:
-                dz_quant(g - 1)
-            h1_quant(g)
-            if g + 2 < GROUPS:
-                h1_interleave(g + 2)
+                out1_pass(g - 2, 2)
+            dz_interleave_pe(scopy if SILC else vcopy, g)
+            dz_interleave(scopy, g, c0, H - 128 * ILW if g < NIL else H)
             if g == last - 1:
-                h1_quant(last)
-                for k in range(5):
-                    out1_pass(k, 2)
+                for k in range(SW):
+                    out1_pass(k, 3)
+            dz_quant(g - 1)
+            dzT_quant(g, 0)
+            h1_quant(g)
+            if g == 1:
+                h1_quant(0)
+                out0_half(1, 0)
 
         g = last
+        h1_step(g)
+        if g - 1 not in TCS:
+            dzT_copy(g - 1, 1)
         dz_compute(g, 0)
         dz_compute(g, 1)
         dzT_transpose(g, 0)
-        dzT_copy(g - 1, 1)
         out0_half(g - 1, 0)
-        for m in range(2):
+        store(g - 1, 0, 2)
+        for m in range(3):
             out1_pass(g - 2, m)
-        dzT_quant(g - 1, 1)
-        dz_quant(g - 1)
-        dz_compute(g, 2)
-        out0_half(g - 1, 1)
-        store(g - 1, 0, J)
-        dzT_copy(g, 0)
-        dz_compute(g, 3)
-        dzT_transpose(g, 1)
-        dz_interleave(scopy, g, 0)
-        dzT_quant(g, 0)
-        out0_half(g, 0)
-        store(g, 0, 2)
-        dz_interleave(vcopy, g, 1)
-        for k in range(5):
+        for k in range(SW, g - 1):
             out1_pass(k, 3)
-        dzT_copy(g, 1)
-        for m in range(2):
+        dz_compute(g, 2)
+        dz_compute(g, 3)
+        dzT_copy(g, 0)
+        dzT_transpose(g, 1)
+        dz_interleave(scopy, g, 0, TI)
+        dzT_quant(g - 1, 1)
+        out0_half(g - 1, 1)
+        store(g - 1, 2, J)
+        dz_quant(g - 1)
+        for m in range(4):
             out1_pass(g - 1, m)
-        for k in (g - 2, g - 1):
-            for m in (2, 3):
-                out1_pass(k, m)
-        dz_quant(g)
+        dzT_quant(g, 0)
+        dzT_copy(g, 1)
+        h1_quant(g)
+        dz_interleave(vcopy, g, TI, H)
         dzT_quant(g, 1)
-        o1 = new([P, 4, H], F32, "o1")
+        dz_quant(g)
+        out0_half(g, 0)
+        store(g, 0, 1)
+        store(g, 1, 2)
+        o1 = new([P, 4, H], F32, "o", OB)
         o1_v = out_1.rearrange("(m p) w -> p m w", p=P)
+
         for m in range(4):
             out1_pass(g, m)
+        for m in range(4):
             if m % 2 == 0:
                 nc.scalar.activation(out=o1[:, m, :], in_=acc[m][:], func=ACT.Copy, scale=0.125)
             else:
                 nc.vector.tensor_scalar(out=o1[:, m, :], in0=acc[m][:], scalar1=0.125, scalar2=None, op0=ALU.mult)
-                nc.sync.dma_start(out=o1_v[:, m - 1:m + 1], in_=o1[:, m - 1:m + 1, :])
+            nc.sync.dma_start(out=o1_v[:, m], in_=o1[:, m, :])
         out0_half(g, 1, emits=(out0_copy_s, out0_copy_v))
-        store(g, 2, 4)
+        store(g, 2, 3)
+        store(g, 3, 4)

@@ -18,16 +18,18 @@ NODES = 512
 EDGES = 4096
 GROUPS = 8
 J = 4
-TCS = (1, 2, 3, 4, 5, 6)
-TI = 256
+TCS = (1, 2, 3, 4, 6)
+TI = 128
 CS = 2
-ILW = 2
-SILC = True
 GS = 4
-NIL = 6
-SW = 4
+SW = 6
+SW6 = 3
+SB = False
+QD = 4
+EV = True
 ZB = 5
 OB = 4
+BANKS = {"acc": 3, "mm": 2, "dh": 1, "trA": 1, "trB": 1}
 FMAX = (2.0 - 2.0 ** -23) * 2.0 ** 127
 
 FLOPS = 2 * H * H * (NODES + EDGES + EDGES)
@@ -53,12 +55,10 @@ def tile_mpnnlayer_pb_v_kernel(tc, h1, h_V, mask_attend, W2, b2, W3, b3, z, grad
             return sb.tile(shape, dtype, name=tag, tag=tag, bufs=bufs, align_bytes=64)
 
         def bank(tag):
-            return ps.tile([P, 512], F32, name=tag, tag=tag, bufs={"acc": 3, "mm": 2}.get(tag, 1))
+            return ps.tile([P, 512], F32, name=tag, tag=tag, bufs=BANKS[tag])
 
         ident = new([P, P], F32, "ident")
         make_identity(nc, ident[:])
-        ident16 = new([P, P], BF16, "ident16")
-        nc.vector.tensor_copy(out=ident16[:], in_=ident[:])
         mk = new([P, H], BF16, "mk")
         nc.vector.memset(mk[:], 0.0)
 
@@ -87,12 +87,12 @@ def tile_mpnnlayer_pb_v_kernel(tc, h1, h_V, mask_attend, W2, b2, W3, b3, z, grad
         nc.sync.dma_start(out=g_raw[:, 0, :], in_=grad_v[:, 0, :])
         nc.sync.dma_start(out=mk[0:GROUPS, :], in_=mask_v)
         load_z(0)
-        nc.sync.dma_start(out=g_raw[:, 1:4, :], in_=grad_v[:, 1:4, :])
+        load_h1(0)
         load_w(w2_raw, w2_v, 0)
         load_w(w2_raw, w2_v, 1)
+        nc.sync.dma_start(out=g_raw[:, 1:4, :], in_=grad_v[:, 1:4, :])
         load_z(1)
         load_h1(1)
-        load_h1(0)
         for g in range(2, ZB):
             load_z(g)
             load_h1(g)
@@ -195,24 +195,11 @@ def tile_mpnnlayer_pb_v_kernel(tc, h1, h_V, mask_attend, W2, b2, W3, b3, z, grad
         w2_codes = new([P, H], U32, "w2_codes")
         w2_scl = new([P, H], U8, "w2_scl")
 
-        last_codes = [None]
-
-        def h1_interleave(on_gpsimd, g):
-            h1i_t[g] = new([P, J * H], BF16, "h1i", 2)
-            out = h1i_t[g][:].rearrange("p (w j) -> p w j", j=J)
-            in_ = h1_t[g][:].rearrange("p j w -> p w j")
-            if on_gpsimd:
-                nc.gpsimd.tensor_scalar(out=out, in0=in_, scalar1=1.0, scalar2=0.0, op0=ALU.mult, op1=ALU.add)
-            else:
-                for k in range(2):
-                    cols = slice(256 * k, 256 * (k + 1))
-                    nc.scalar.copy(out=out[:, cols], in_=in_[:, cols])
-
-        token = new([P, 1], U32, "token")
-
-        def h1_step(g):
-            nc.gpsimd.tensor_copy(out=token[:], in_=last_codes[0][:, 0:1])
-            h1_interleave(True, g)
+        def h1_interleave(g):
+            h1i_t[g] = new([P, J * H], BF16, "h1i", 1)
+            nc.gpsimd.tensor_scalar(
+                out=h1i_t[g][:].rearrange("p (w j) -> p w j", j=J), in0=h1_t[g][:].rearrange("p j w -> p w j"),
+                scalar1=1.0, scalar2=0.0, op0=ALU.mult, op1=ALU.add)
 
         def h1_quant(g):
             h1c_t[g] = new([P, H], U32, "h1c", 8)
@@ -227,20 +214,6 @@ def tile_mpnnlayer_pb_v_kernel(tc, h1, h_V, mask_attend, W2, b2, W3, b3, z, grad
                 in1=dh_t[g][:], op0=ALU.is_gt, op1=ALU.mult,
             )
 
-        def dz_interleave_pe(copy, g):
-            lo = H - 128 * ILW
-            if ILW == 0 or g >= NIL:
-                return
-            bk = ps.tile([P, 1024], BF16, name="il", tag="il", bufs=1)
-            for k in range(ILW):
-                w0 = lo + 128 * k
-                nc.tensor.matmul(
-                    out=bk[:, 512 * k:512 * (k + 1)], lhsT=ident16[:],
-                    rhs=dz_t[g][:, :, w0:w0 + 128].rearrange("p j w -> p w j"),
-                    start=True, stop=True,
-                )
-            copy(out=dzi_t[g][:, 4 * lo:4 * H], in_=bk[:, 0:512 * ILW])
-
         def dz_interleave(copy, g, lo, hi):
             if hi == lo:
                 return
@@ -248,10 +221,10 @@ def tile_mpnnlayer_pb_v_kernel(tc, h1, h_V, mask_attend, W2, b2, W3, b3, z, grad
                 dzi_t[g] = new([P, J * H], BF16, "dzi", 2)
             out = dzi_t[g][:].rearrange("p (w j) -> p w j", j=J)[:, lo:hi, :]
             in_ = dz_t[g][:].rearrange("p j w -> p w j")[:, lo:hi, :]
-            if copy == "g":
-                nc.gpsimd.tensor_scalar(out=out, in0=in_, scalar1=1.0, scalar2=0.0, op0=ALU.mult, op1=ALU.add)
-            else:
-                copy(out=out, in_=in_)
+            copy(
+                out=out.rearrange("p (c i) j -> p c j i", i=4),
+                in_=in_.rearrange("p (c i) j -> p c j i", i=4),
+            )
 
         def dz_quant(g):
             dzc_t[g] = new([P, H], U32, "dzc", 8)
@@ -259,7 +232,7 @@ def tile_mpnnlayer_pb_v_kernel(tc, h1, h_V, mask_attend, W2, b2, W3, b3, z, grad
             nc.vector.quantize_mx(out=dzc_t[g][:].bitcast(E5M2), scales=dzs_t[g][:], in_=dzi_t[g][:])
 
         def dzT_transpose(g, h):
-            bk = bank("tr")
+            bk = bank("trB" if h == 1 and g < GROUPS - 2 else "trA")
             tr_t[g, h] = bk[:].rearrange("p (v u r) -> p v u r", u=2, r=P)
             for v in range(2):
                 transpose_words(tr_t[g, h][:, v], words_of(dz_t[g], 2 * h + v))
@@ -275,7 +248,6 @@ def tile_mpnnlayer_pb_v_kernel(tc, h1, h_V, mask_attend, W2, b2, W3, b3, z, grad
             tc_t[g, h] = new([P, 2 * P], U32, "tcod", 3)
             ts_t[g, h] = new([P, 2 * P], U8, "tscl", 3)
             nc.vector.quantize_mx(out=tc_t[g, h][:].bitcast(E5M2), scales=ts_t[g, h][:], in_=dzT_t[g, h][:])
-            last_codes[0] = tc_t[g, h]
 
         def out0_matmul(g, h, v):
             bk = bank("mm")
@@ -305,7 +277,7 @@ def tile_mpnnlayer_pb_v_kernel(tc, h1, h_V, mask_attend, W2, b2, W3, b3, z, grad
 
         def out1_pass(g, m):
             if g == 0:
-                acc[m] = bank("acc" if m < 3 else "il")
+                acc[m] = bank("acc" if m < 3 else "trB")
             cols = slice(P * m, P * (m + 1))
             nc.tensor.matmul_mx(
                 out=acc[m][:],
@@ -320,47 +292,45 @@ def tile_mpnnlayer_pb_v_kernel(tc, h1, h_V, mask_attend, W2, b2, W3, b3, z, grad
         def store(g, lo, hi):
             nc.sync.dma_start(out=o_v[:, g, lo:hi], in_=o_t[g][:, lo:hi, :])
 
+        w2_t = new([P, J * H], BF16, "w2_t")
+        h1_interleave(0)
         dz_compute(0, 0)
         dz_compute(0, 1)
-        for t in (1, 2, 3):
-            gts[t] = g_copy(scopy if t < GS else vcopy, g_tile(), g_transpose(t, "acc"), 2)
         dzT_transpose(0, 0)
-        w2_t = new([P, J * H], BF16, "w2_t")
-        for b in range(2):
-            w_copy(scopy if b < CS else vcopy, w2_t, b, w_bank(w2_raw, b, "mm"))
+        w_copy(scopy, w2_t, 0, w_bank(w2_raw, 0, "mm"))
         dz_compute(0, 2)
-        dzT_copy(0, 0)
-        g_quant(0, gt0, 1)
         dz_compute(0, 3)
+        w_copy(scopy, w2_t, 1, w_bank(w2_raw, 1, "mm"))
+        dz_interleave(scopy, 0, 0, 256)
+        g_quant(0, gt0, 1)
         dh_matmul(1)
         dzT_transpose(0, 1)
+        h1_quant(0)
+        dzT_copy(0, 0)
         load_z(ZB)
         load_h1(ZB)
-        dz_interleave(scopy, 0, 0, c0)
-        dz_interleave_pe(scopy, 0)
-        dzT_quant(0, 0)
         for b in range(2):
             w_quant(w2_codes, w2_scl, w2_t, b)
+        dzT_quant(0, 0)
+        gts[1] = g_copy(scopy, g_tile(), g_transpose(1, "acc"), 2)
         out0_half(0, 0)
-        g_quant(1, gts[1], 2)
         dzT_copy(0, 1)
-        dz_interleave(scopy, 0, c0, H - 128 * ILW)
-        for t in (2, 3):
-            g_quant(t, gts[t], 2)
+        g_quant(1, gts[1], 2)
         dzT_quant(0, 1)
+        dz_interleave(scopy, 0, 256, H)
+        for t in (2, 3):
+            gts[t] = g_copy(scopy, g_tile(), g_transpose(t, "acc"), 2)
         out0_half(0, 1)
         store(0, 0, J)
-        h1_interleave(False, 0)
 
         for g in range(1, last):
-            prev1 = g > 1
-            h1_step(g)
-            if prev1 and g - 1 not in TCS:
+            h1_interleave(g)
+            if g > 1 and g - 1 not in TCS:
                 dzT_copy(g - 1, 1)
             dz_compute(g, 0)
             dz_compute(g, 1)
             dzT_transpose(g, 0)
-            if prev1:
+            if g > 1:
                 if g > 2:
                     out0_half(g - 1, 0)
                 for m in range(2):
@@ -370,30 +340,30 @@ def tile_mpnnlayer_pb_v_kernel(tc, h1, h_V, mask_attend, W2, b2, W3, b3, z, grad
             dzT_copy(g, 0)
             dh_matmul(g + 1)
             dzT_transpose(g, 1)
-            dz_interleave(scopy, g, 0, c0)
+            dz_interleave(scopy, g, 0, 256)
             if g in TCS:
                 dzT_copy(g, 1)
             load_z(g + ZB)
             load_h1(g + ZB)
-            if prev1:
+            if g > 1:
                 dzT_quant(g - 1, 1)
                 out0_half(g - 1, 1)
                 store(g - 1, 0, J)
                 out1_pass(g - 2, 2)
-            dz_interleave_pe(scopy if SILC else vcopy, g)
-            dz_interleave(scopy, g, c0, H - 128 * ILW if g < NIL else H)
             if g == last - 1:
-                for k in range(SW):
+                for k in range(SW6):
                     out1_pass(k, 3)
+            dz_interleave(scopy, g, 256, H)
             dz_quant(g - 1)
             dzT_quant(g, 0)
             h1_quant(g)
             if g == 1:
-                h1_quant(0)
+                for t in (2, 3):
+                    g_quant(t, gts[t], 2)
                 out0_half(1, 0)
 
         g = last
-        h1_step(g)
+        h1_interleave(g)
         if g - 1 not in TCS:
             dzT_copy(g - 1, 1)
         dz_compute(g, 0)
@@ -403,31 +373,41 @@ def tile_mpnnlayer_pb_v_kernel(tc, h1, h_V, mask_attend, W2, b2, W3, b3, z, grad
         store(g - 1, 0, 2)
         for m in range(3):
             out1_pass(g - 2, m)
-        for k in range(SW, g - 1):
-            out1_pass(k, 3)
+        if SB:
+            for k in range(SW6, SW):
+                out1_pass(k, 3)
         dz_compute(g, 2)
         dz_compute(g, 3)
         dzT_copy(g, 0)
         dzT_transpose(g, 1)
-        dz_interleave(scopy, g, 0, TI)
         dzT_quant(g - 1, 1)
         out0_half(g - 1, 1)
         store(g - 1, 2, J)
-        dz_quant(g - 1)
-        for m in range(4):
-            out1_pass(g - 1, m)
         dzT_quant(g, 0)
+        if not SB:
+            for k in range(SW6, SW):
+                out1_pass(k, 3)
+        dz_interleave(scopy, g, 0, TI)
         dzT_copy(g, 1)
-        h1_quant(g)
-        dz_interleave(vcopy, g, TI, H)
-        dzT_quant(g, 1)
-        dz_quant(g)
         out0_half(g, 0)
         store(g, 0, 1)
         store(g, 1, 2)
+        for k in range(SW, g - 1):
+            out1_pass(k, 3)
+        dz_quant(g - 1)
+        dzT_quant(g, 1)
+        for m in range(QD):
+            out1_pass(g - 1, m)
+        h1_quant(g)
+        dz_interleave(vcopy, g, TI, H)
+        dz_quant(g)
+        out0_half(g, 1, emits=(out0_copy_s, out0_copy_v) if EV else None)
+        store(g, 2, 3)
+        store(g, 3, 4)
+        for m in range(QD, 4):
+            out1_pass(g - 1, m)
         o1 = new([P, 4, H], F32, "o", OB)
         o1_v = out_1.rearrange("(m p) w -> p m w", p=P)
-
         for m in range(4):
             out1_pass(g, m)
         for m in range(4):
@@ -436,6 +416,3 @@ def tile_mpnnlayer_pb_v_kernel(tc, h1, h_V, mask_attend, W2, b2, W3, b3, z, grad
             else:
                 nc.vector.tensor_scalar(out=o1[:, m, :], in0=acc[m][:], scalar1=0.125, scalar2=None, op0=ALU.mult)
             nc.sync.dma_start(out=o1_v[:, m], in_=o1[:, m, :])
-        out0_half(g, 1, emits=(out0_copy_s, out0_copy_v))
-        store(g, 2, 3)
-        store(g, 3, 4)

from contextlib import ExitStack

import concourse.mybir as mybir
from concourse.masks import make_identity

F32 = mybir.dt.float32
BF16 = mybir.dt.bfloat16
U32 = mybir.dt.uint32
U8 = mybir.dt.uint8
E4M3 = mybir.dt.float8_e4m3fn_x4
E5M2 = mybir.dt.float8_e5m2_x4
ALU = mybir.AluOpType
ACT = mybir.ActivationFunctionType

P = 128
H = 512
NODES = 512
EDGES = 4096
GROUPS = 8
J = 4
TCS = (1, 2, 3, 4, 6)
TI = 128
CS = 2
GS = 4
SW = 6
SW6 = 3
SB = False
QD = 4
EV = True
ZB = 5
OB = 4
BANKS = {"acc": 3, "mm": 2, "dh": 1, "trA": 1, "trB": 1}
FMAX = (2.0 - 2.0 ** -23) * 2.0 ** 127

FLOPS = 2 * H * H * (NODES + EDGES + EDGES)
BYTES = 2 * (EDGES * H + EDGES + 2 * H * H + NODES * H) + 4 * (EDGES * H + EDGES * H + H * H)


def tile_mpnnlayer_pb_v_kernel(tc, h1, h_V, mask_attend, W2, b2, W3, b3, z, grad_out, out_0, out_1):
    nc = tc.nc
    h1_v = h1.rearrange("b n k w -> (b n k) w").rearrange("(g p j) w -> p g j w", p=P, j=J)
    z_v = z.rearrange("b n k w -> (b n k) w").rearrange("(g p j) w -> p g j w", p=P, j=J)
    o_v = out_0.rearrange("b n k w -> (b n k) w").rearrange("(g p j) w -> p g j w", p=P, j=J)
    mask_v = mask_attend.rearrange("b n k -> (b n k)").rearrange("(g c) -> g c", g=GROUPS)
    grad_v = grad_out.rearrange("b n w -> (b n) w").rearrange("(t p) w -> p t w", p=P)
    w2_v = W2.rearrange("(b r v) w -> r b v w", b=2, v=2)
    w3_v = W3.rearrange("(b r v) w -> r b v w", b=2, v=2)

    with ExitStack() as ctx:
        ctx.enter_context(tc.manual_schedule())
        sb = ctx.enter_context(tc.tile_pool(name="sb", bufs=1))
        ps = ctx.enter_context(tc.psum_pool(name="ps", bufs=2))

        def new(shape, dtype, tag, bufs=1):
            return sb.tile(shape, dtype, name=tag, tag=tag, bufs=bufs, align_bytes=64)

        def bank(tag):
            return ps.tile([P, 512], F32, name=tag, tag=tag, bufs=BANKS[tag])

        ident = new([P, P], F32, "ident")
        make_identity(nc, ident[:])
        mk = new([P, H], BF16, "mk")
        nc.vector.memset(mk[:], 0.0)

        g_raw = new([P, 4, H], BF16, "g_raw")
        w3_raw = new([P, J, H], BF16, "w3_raw")
        w2_raw = new([P, J, H], BF16, "w2_raw")

        def load_w(raw, view, b):
            nc.sync.dma_start(out=raw[:, 2 * b:2 * b + 2, :], in_=view[:, b])

        z_t = {}
        h1_t = {}

        def load_z(g):
            if g < GROUPS:
                z_t[g] = new([P, J, H], F32, "z", ZB)
                nc.sync.dma_start(out=z_t[g][:], in_=z_v[:, g])

        def load_h1(g):
            if g < GROUPS:
                h1_t[g] = new([P, J, H], BF16, "h1", ZB)
                nc.sync.dma_start(out=h1_t[g][:], in_=h1_v[:, g])

        load_w(w3_raw, w3_v, 0)
        load_w(w3_raw, w3_v, 1)
        nc.sync.dma_start(out=g_raw[:, 0, :], in_=grad_v[:, 0, :])
        nc.sync.dma_start(out=mk[0:GROUPS, :], in_=mask_v)
        load_z(0)
        load_h1(0)
        load_w(w2_raw, w2_v, 0)
        load_w(w2_raw, w2_v, 1)
        nc.sync.dma_start(out=g_raw[:, 1:4, :], in_=grad_v[:, 1:4, :])
        load_z(1)
        load_h1(1)
        for g in range(2, ZB):
            load_z(g)
            load_h1(g)

        def transpose_words(dst, words):
            for u in range(2):
                nc.tensor.transpose(dst[:, u, :], words[:, u:256:2], ident[:])

        def words_of(tile3, j):
            return tile3[:, j, :].bitcast(F32)

        g_codes = new([P, 2 * NODES], U32, "g_codes")
        g_scl = new([P, 2 * NODES], U8, "g_scl")

        def g_transpose(t, tag):
            b = bank(tag)
            bv = b[:].rearrange("p (v u r) -> p v u r", u=2, r=P)
            transpose_words(bv[:, 0], words_of(g_raw, t))
            return bv

        def g_tile():
            return new([P, 2 * P * 4], BF16, "gt", 4)

        def g_copy(copy, gt, bv, half):
            rows = slice(64 * half, 64 * half + 64) if half < 2 else slice(0, P)
            n = P if half == 2 else 64
            copy(
                out=gt[:].bitcast(F32).rearrange("p (r d u) -> p r d u", d=2, u=2)[:, rows],
                in_=bv[:, 0, :, rows].rearrange("p u r -> p r u").unsqueeze(2).to_broadcast([P, n, 2, 2]),
            )
            return gt

        def g_quant(t, gt, half):
            lo, hi = (0, 256) if half == 2 else (128 * half, 128 * half + 128)
            nc.vector.quantize_mx(
                out=g_codes[:, 256 * t + lo:256 * t + hi].bitcast(E5M2), scales=g_scl[:, 256 * t + lo:256 * t + hi],
                in_=gt[:, 4 * lo:4 * hi])

        def w_bank(raw, b, tag):
            bk = bank(tag)
            bv = bk[:].rearrange("p (v u r) -> p v u r", u=2, r=P)
            for v in range(2):
                transpose_words(bv[:, v], words_of(raw, 2 * b + v))
            return bv

        def w_copy(copy, dst, b, bv):
            copy(
                out=dst[:].bitcast(F32).rearrange("p (b r v u) -> p b r v u", b=2, v=2, u=2)[:, b],
                in_=bv.rearrange("p v u r -> p r v u"),
            )

        def w_quant(codes, scl, dst, b):
            cols = slice(256 * b, 256 * (b + 1))
            nc.vector.quantize_mx(out=codes[:, cols].bitcast(E4M3), scales=scl[:, cols], in_=dst[:, 1024 * b:1024 * (b + 1)])

        vcopy = nc.vector.tensor_copy
        scopy = nc.scalar.copy

        w3_t = new([P, J * H], BF16, "w3_t")
        w3_codes = new([P, H], U32, "w3_codes")
        w3_scl = new([P, H], U8, "w3_scl")
        w_copy(scopy, w3_t, 0, w_bank(w3_raw, 0, "mm"))
        w_copy(vcopy, w3_t, 1, w_bank(w3_raw, 1, "mm"))
        gb0 = g_transpose(0, "acc")
        gt0 = g_tile()
        g_copy(scopy, gt0, gb0, 0)
        mb = bank("acc")
        mv = mb[:].rearrange("p (v u r) -> p v u r", u=2, r=P)
        transpose_words(mv[:, 0], mk[:].bitcast(F32))
        w_quant(w3_codes, w3_scl, w3_t, 0)
        w_quant(w3_codes, w3_scl, w3_t, 1)
        g_quant(0, gt0, 0)
        m_t = new([P, GROUPS * J], BF16, "m_t")
        vcopy(
            out=m_t[:].bitcast(F32).rearrange("p (g u) -> p g u", u=2),
            in_=mv[:, 0, :, 0:GROUPS].rearrange("p u g -> p g u"),
        )
        thr = new([P, GROUPS * J], F32, "thr")
        nc.vector.tensor_scalar(out=thr[:], in0=m_t[:], scalar1=-FMAX, scalar2=FMAX, op0=ALU.mult, op1=ALU.add)

        dh_t = {}

        def dh_matmul(g):
            if g < GROUPS:
                dh_t[g] = bank("dh")
                cols = slice(P * g, P * (g + 1))
                nc.tensor.matmul_mx(
                    out=dh_t[g][:],
                    lhsT=g_codes[:, cols].bitcast(E5M2), lhsT_scale=g_scl[:, cols],
                    rhs=w3_codes[:].bitcast(E4M3), rhs_scale=w3_scl[:],
                    start=True, stop=True,
                )

        dh_matmul(0)
        g_copy(scopy, gt0, gb0, 1)
        gts = {}

        dz_t, dzi_t, dzc_t, dzs_t, h1i_t, h1c_t, h1s_t = {}, {}, {}, {}, {}, {}, {}
        tr_t, dzT_t, tc_t, ts_t, o_t = {}, {}, {}, {}, {}
        w2_codes = new([P, H], U32, "w2_codes")
        w2_scl = new([P, H], U8, "w2_scl")

        def h1_interleave(g):
            h1i_t[g] = new([P, J * H], BF16, "h1i", 1)
            nc.gpsimd.tensor_scalar(
                out=h1i_t[g][:].rearrange("p (w j) -> p w j", j=J), in0=h1_t[g][:].rearrange("p j w -> p w j"),
                scalar1=1.0, scalar2=0.0, op0=ALU.mult, op1=ALU.add)

        def h1_quant(g):
            h1c_t[g] = new([P, H], U32, "h1c", 8)
            h1s_t[g] = new([P, H], U8, "h1s", 8)
            nc.vector.quantize_mx(out=h1c_t[g][:].bitcast(E4M3), scales=h1s_t[g][:], in_=h1i_t[g][:])

        def dz_compute(g, j):
            if j == 0:
                dz_t[g] = new([P, J, H], BF16, "dz", 3)
            nc.vector.scalar_tensor_tensor(
                out=dz_t[g][:, j, :], in0=z_t[g][:, j, :], scalar=thr[:, J * g + j:J * g + j + 1],
                in1=dh_t[g][:], op0=ALU.is_gt, op1=ALU.mult,
            )

        def dz_interleave(copy, g, lo, hi):
            if hi == lo:
                return
            if g not in dzi_t:
                dzi_t[g] = new([P, J * H], BF16, "dzi", 2)
            out = dzi_t[g][:].rearrange("p (w j) -> p w j", j=J)[:, lo:hi, :]
            in_ = dz_t[g][:].rearrange("p j w -> p w j")[:, lo:hi, :]
            copy(
                out=out.rearrange("p (c i) j -> p c j i", i=4),
                in_=in_.rearrange("p (c i) j -> p c j i", i=4),
            )

        def dz_quant(g):
            dzc_t[g] = new([P, H], U32, "dzc", 8)
            dzs_t[g] = new([P, H], U8, "dzs", 8)
            nc.vector.quantize_mx(out=dzc_t[g][:].bitcast(E5M2), scales=dzs_t[g][:], in_=dzi_t[g][:])

        def dzT_transpose(g, h):
            bk = bank("trB" if h == 1 and g < GROUPS - 2 else "trA")
            tr_t[g, h] = bk[:].rearrange("p (v u r) -> p v u r", u=2, r=P)
            for v in range(2):
                transpose_words(tr_t[g, h][:, v], words_of(dz_t[g], 2 * h + v))

        def dzT_copy(g, h):
            dzT_t[g, h] = new([P, 2 * P * 4], BF16, "dzT", 3)
            (scopy if h == 1 and g in TCS else vcopy)(
                out=dzT_t[g, h][:].bitcast(F32).rearrange("p (v r u) -> p v r u", r=P, u=2),
                in_=tr_t[g, h].rearrange("p v u r -> p v r u"),
            )

        def dzT_quant(g, h):
            tc_t[g, h] = new([P, 2 * P], U32, "tcod", 3)
            ts_t[g, h] = new([P, 2 * P], U8, "tscl", 3)
            nc.vector.quantize_mx(out=tc_t[g, h][:].bitcast(E5M2), scales=ts_t[g, h][:], in_=dzT_t[g, h][:])

        def out0_matmul(g, h, v):
            bk = bank("mm")
            cols = slice(P * v, P * (v + 1))
            nc.tensor.matmul_mx(
                out=bk[:],
                lhsT=tc_t[g, h][:, cols].bitcast(E5M2), lhsT_scale=ts_t[g, h][:, cols],
                rhs=w2_codes[:].bitcast(E4M3), rhs_scale=w2_scl[:],
                start=True, stop=True,
            )
            return bk

        def out0_copy_s(g, h, v, bk):
            nc.scalar.activation(out=o_t[g][:, 2 * h + v, :], in_=bk[:], func=ACT.Copy, scale=0.125)

        def out0_copy_v(g, h, v, bk):
            nc.vector.tensor_scalar(out=o_t[g][:, 2 * h + v, :], in0=bk[:], scalar1=0.125, scalar2=None, op0=ALU.mult)

        def out0_half(g, h, emits=None):
            if h == 0:
                o_t[g] = new([P, J, H], F32, "o", OB)
            banks = [out0_matmul(g, h, v) for v in range(2)]
            for v in range(2):
                (out0_copy_s if emits is None else emits[v])(g, h, v, banks[v])

        acc = {}

        def out1_pass(g, m):
            if g == 0:
                acc[m] = bank("acc" if m < 3 else "trB")
            cols = slice(P * m, P * (m + 1))
            nc.tensor.matmul_mx(
                out=acc[m][:],
                lhsT=h1c_t[g][:, cols].bitcast(E4M3), lhsT_scale=h1s_t[g][:, cols],
                rhs=dzc_t[g][:].bitcast(E5M2), rhs_scale=dzs_t[g][:],
                start=(g == 0), stop=(g == GROUPS - 1),
            )

        last = GROUPS - 1
        c0 = 256

        def store(g, lo, hi):
            nc.sync.dma_start(out=o_v[:, g, lo:hi], in_=o_t[g][:, lo:hi, :])

        w2_t = new([P, J * H], BF16, "w2_t")
        h1_interleave(0)
        dz_compute(0, 0)
        dz_compute(0, 1)
        dzT_transpose(0, 0)
        w_copy(scopy, w2_t, 0, w_bank(w2_raw, 0, "mm"))
        dz_compute(0, 2)
        dz_compute(0, 3)
        w_copy(scopy, w2_t, 1, w_bank(w2_raw, 1, "mm"))
        dz_interleave(scopy, 0, 0, 256)
        g_quant(0, gt0, 1)
        dh_matmul(1)
        dzT_transpose(0, 1)
        h1_quant(0)
        dzT_copy(0, 0)
        load_z(ZB)
        load_h1(ZB)
        for b in range(2):
            w_quant(w2_codes, w2_scl, w2_t, b)
        dzT_quant(0, 0)
        gts[1] = g_copy(scopy, g_tile(), g_transpose(1, "acc"), 2)
        out0_half(0, 0)
        dzT_copy(0, 1)
        g_quant(1, gts[1], 2)
        dzT_quant(0, 1)
        dz_interleave(scopy, 0, 256, H)
        for t in (2, 3):
            gts[t] = g_copy(scopy, g_tile(), g_transpose(t, "acc"), 2)
        out0_half(0, 1)
        store(0, 0, J)

        for g in range(1, last):
            h1_interleave(g)
            if g > 1 and g - 1 not in TCS:
                dzT_copy(g - 1, 1)
            dz_compute(g, 0)
            dz_compute(g, 1)
            dzT_transpose(g, 0)
            if g > 1:
                if g > 2:
                    out0_half(g - 1, 0)
                for m in range(2):
                    out1_pass(g - 2, m)
            dz_compute(g, 2)
            dz_compute(g, 3)
            dzT_copy(g, 0)
            dh_matmul(g + 1)
            dzT_transpose(g, 1)
            dz_interleave(scopy, g, 0, 256)
            if g in TCS:
                dzT_copy(g, 1)
            load_z(g + ZB)
            load_h1(g + ZB)
            if g > 1:
                dzT_quant(g - 1, 1)
                out0_half(g - 1, 1)
                store(g - 1, 0, J)
                out1_pass(g - 2, 2)
            if g == last - 1:
                for k in range(SW6):
                    out1_pass(k, 3)
            dz_interleave(scopy, g, 256, H)
            dz_quant(g - 1)
            dzT_quant(g, 0)
            h1_quant(g)
            if g == 1:
                for t in (2, 3):
                    g_quant(t, gts[t], 2)
                out0_half(1, 0)

        g = last
        h1_interleave(g)
        if g - 1 not in TCS:
            dzT_copy(g - 1, 1)
        dz_compute(g, 0)
        dz_compute(g, 1)
        dzT_transpose(g, 0)
        out0_half(g - 1, 0)
        store(g - 1, 0, 2)
        for m in range(3):
            out1_pass(g - 2, m)
        if SB:
            for k in range(SW6, SW):
                out1_pass(k, 3)
        dz_compute(g, 2)
        dz_compute(g, 3)
        dzT_copy(g, 0)
        dzT_transpose(g, 1)
        dzT_quant(g - 1, 1)
        out0_half(g - 1, 1)
        store(g - 1, 2, J)
        dzT_quant(g, 0)
        if not SB:
            for k in range(SW6, SW):
                out1_pass(k, 3)
        dz_interleave(scopy, g, 0, TI)
        dzT_copy(g, 1)
        out0_half(g, 0)
        store(g, 0, 1)
        store(g, 1, 2)
        for k in range(SW, g - 1):
            out1_pass(k, 3)
        dz_quant(g - 1)
        dzT_quant(g, 1)
        for m in range(QD):
            out1_pass(g - 1, m)
        h1_quant(g)
        dz_interleave(vcopy, g, TI, H)
        dz_quant(g)
        out0_half(g, 1, emits=(out0_copy_s, out0_copy_v) if EV else None)
        store(g, 2, 3)
        store(g, 3, 4)
        for m in range(QD, 4):
            out1_pass(g - 1, m)
        o1 = new([P, 4, H], F32, "o", OB)
        o1_v = out_1.rearrange("(m p) w -> p m w", p=P)
        for m in range(4):
            out1_pass(g, m)
        for m in range(4):
            if m % 2 == 0:
                nc.scalar.activation(out=o1[:, m, :], in_=acc[m][:], func=ACT.Copy, scale=0.125)
            else:
                nc.vector.tensor_scalar(out=o1[:, m, :], in0=acc[m][:], scalar1=0.125, scalar2=None, op0=ALU.mult)
            nc.sync.dma_start(out=o1_v[:, m], in_=o1[:, m, :])
